import numpy as np
import ml_dtypes

BF16 = ml_dtypes.bfloat16


def bf(x):
    return np.asarray(x, np.float32).astype(BF16)


def f32(x):
    return np.asarray(x, np.float32)


def f64(x):
    return np.asarray(x).astype(np.float64)


def striped(idx):
    return np.tile(idx.reshape(-1, 16).T, (8, 1))


E, D, DF, V, M, N = 128, 128, 32, 512, 256, 1024


def setup_inputs():
    fixed = np.random.standard_normal((DF, N))
    nanflag = np.random.uniform(size=(DF, N))
    dyn = np.random.standard_normal((DF, N))
    weather = np.random.standard_normal((DF, N))
    return {"table": bf(np.random.standard_normal((E, V))), "w_emb": bf(np.random.standard_normal((E, M)) / np.sqrt(E)), "feats": bf(np.concatenate([fixed, nanflag, dyn, weather], axis=0)), "w_feat": bf(np.random.standard_normal((D, M)) / np.sqrt(D)), "b": f32(0.1 * np.random.standard_normal((M, 1))), "offs": striped(np.random.permutation(np.tile(np.arange(V), 2))[:N])}


def reference(table, w_emb, feats, w_feat, b, offs):
    idx = offs[:16].T.reshape(-1)
    return f64(w_emb).T @ f64(table)[:, idx] + f64(w_feat).T @ f64(feats) + f64(b)

@@ -1,0 +1,56 @@
+import concourse.mybir as mybir
+
+BF16, F32, U16 = mybir.dt.bfloat16, mybir.dt.float32, mybir.dt.uint16
+
+P = 128
+STATIONS = 512
+M = 256
+N = 1024
+PIECE = 512
+PER_COLUMN = 16
+
+FLOPS = 2 * M * N * (P + P)
+
+
+def tile_spaceattn_kernel(tc, table, w_emb, feats, w_feat, b, offs, out):
+    nc = tc.nc
+    with (
+        tc.tile_pool(name="held", bufs=1) as held,
+        tc.tile_pool(name="results", bufs=4) as results,
+        tc.psum_pool(name="banks", bufs=1) as banks,
+    ):
+        offsets = held.tile([P, N // PER_COLUMN], U16, name="offsets")
+        nc.sync.dma_start(offsets[:], offs)
+        w_emb_sb = held.tile([P, M], BF16, name="w_emb_sb")
+        nc.scalar.dma_start(w_emb_sb[:], w_emb)
+        table_sb = held.tile([P, STATIONS], BF16, name="table_sb")
+        nc.sync.dma_start(table_sb[:], table)
+        w_feat_sb = held.tile([P, M], BF16, name="w_feat_sb")
+        nc.scalar.dma_start(w_feat_sb[:], w_feat)
+        feats_sb = held.tile([P, N], BF16, name="feats_sb")
+        nc.sync.dma_start(feats_sb[:], feats)
+        bias = [held.tile([P, 1], F32, name=f"bias{h}") for h in range(M // P)]
+        for h in range(M // P):
+            nc.scalar.dma_start(bias[h][:], b[h * P : (h + 1) * P, :])
+
+        blocks = [(piece, h) for piece in range(N // PIECE) for h in range(M // P)]
+        bank = {block: banks.tile([P, PIECE], F32, name=f"bank{block[0]}{block[1]}") for block in blocks}
+
+        for piece, h in blocks:
+            piece_offsets = offsets[:, piece * (PIECE // PER_COLUMN) : (piece + 1) * (PIECE // PER_COLUMN)]
+            nc.tensor.matmul(
+                bank[piece, h][:],
+                w_emb_sb[:, h * P : (h + 1) * P],
+                table_sb[:].indirect(piece_offsets),
+                start=True,
+                stop=False,
+            )
+        for piece, h in blocks:
+            rows = slice(h * P, (h + 1) * P)
+            positions = slice(piece * PIECE, (piece + 1) * PIECE)
+            nc.tensor.matmul(bank[piece, h][:], w_feat_sb[:, rows], feats_sb[:, positions], start=False, stop=True)
+            result = results.tile([P, PIECE], F32, name="result")
+            nc.vector.tensor_scalar(
+                out=result[:], in0=bank[piece, h][:], scalar1=bias[h][:], scalar2=None, op0=mybir.AluOpType.add
+            )
+            nc.sync.dma_start(out[rows, positions], result[:])

@@ -6,7 +6,7 @@ P = 128
 STATIONS = 512
 M = 256
 N = 1024
-PIECE = 512
+PIECE = 256
 PER_COLUMN = 16
 
 FLOPS = 2 * M * N * (P + P)
@@ -19,16 +19,16 @@ def tile_spaceattn_kernel(tc, table, w_emb, feats, w_feat, b, offs, out):
         tc.tile_pool(name="results", bufs=4) as results,
         tc.psum_pool(name="banks", bufs=1) as banks,
     ):
+        w_feat_sb = held.tile([P, M], BF16, name="w_feat_sb")
+        nc.scalar.dma_start(w_feat_sb[:], w_feat)
+        feats_sb = held.tile([P, N], BF16, name="feats_sb")
+        nc.sync.dma_start(feats_sb[:], feats)
         offsets = held.tile([P, N // PER_COLUMN], U16, name="offsets")
         nc.sync.dma_start(offsets[:], offs)
         w_emb_sb = held.tile([P, M], BF16, name="w_emb_sb")
         nc.scalar.dma_start(w_emb_sb[:], w_emb)
         table_sb = held.tile([P, STATIONS], BF16, name="table_sb")
         nc.sync.dma_start(table_sb[:], table)
-        w_feat_sb = held.tile([P, M], BF16, name="w_feat_sb")
-        nc.scalar.dma_start(w_feat_sb[:], w_feat)
-        feats_sb = held.tile([P, N], BF16, name="feats_sb")
-        nc.sync.dma_start(feats_sb[:], feats)
         bias = [held.tile([P, 1], F32, name=f"bias{h}") for h in range(M // P)]
         for h in range(M // P):
             nc.scalar.dma_start(bias[h][:], b[h * P : (h + 1) * P, :])
@@ -37,20 +37,24 @@ def tile_spaceattn_kernel(tc, table, w_emb, feats, w_feat, b, offs, out):
         bank = {block: banks.tile([P, PIECE], F32, name=f"bank{block[0]}{block[1]}") for block in blocks}
 
         for piece, h in blocks:
+            nc.tensor.matmul(
+                bank[piece, h][:],
+                w_feat_sb[:, h * P : (h + 1) * P],
+                feats_sb[:, piece * PIECE : (piece + 1) * PIECE],
+                start=True,
+                stop=False,
+            )
+        for piece, h in blocks:
             piece_offsets = offsets[:, piece * (PIECE // PER_COLUMN) : (piece + 1) * (PIECE // PER_COLUMN)]
             nc.tensor.matmul(
                 bank[piece, h][:],
                 w_emb_sb[:, h * P : (h + 1) * P],
                 table_sb[:].indirect(piece_offsets),
-                start=True,
-                stop=False,
+                start=False,
+                stop=True,
             )
-        for piece, h in blocks:
-            rows = slice(h * P, (h + 1) * P)
-            positions = slice(piece * PIECE, (piece + 1) * PIECE)
-            nc.tensor.matmul(bank[piece, h][:], w_feat_sb[:, rows], feats_sb[:, positions], start=False, stop=True)
             result = results.tile([P, PIECE], F32, name="result")
             nc.vector.tensor_scalar(
                 out=result[:], in0=bank[piece, h][:], scalar1=bias[h][:], scalar2=None, op0=mybir.AluOpType.add
             )
-            nc.sync.dma_start(out[rows, positions], result[:])
+            nc.sync.dma_start(out[h * P : (h + 1) * P, piece * PIECE : (piece + 1) * PIECE], result[:])

@@ -8,41 +8,45 @@ M = 256
 N = 1024
 PIECE = 256
 PER_COLUMN = 16
+WARM_UPS = 5
 
 FLOPS = 2 * M * N * (P + P)
 
 
 def tile_spaceattn_kernel(tc, table, w_emb, feats, w_feat, b, offs, out):
     nc = tc.nc
+    pieces, halves = range(N // PIECE), range(M // P)
     with (
         tc.tile_pool(name="held", bufs=1) as held,
-        tc.tile_pool(name="results", bufs=4) as results,
         tc.psum_pool(name="banks", bufs=1) as banks,
     ):
         w_feat_sb = held.tile([P, M], BF16, name="w_feat_sb")
         nc.scalar.dma_start(w_feat_sb[:], w_feat)
-        feats_sb = held.tile([P, N], BF16, name="feats_sb")
-        nc.sync.dma_start(feats_sb[:], feats)
+        feats_sb = [held.tile([P, PIECE], BF16, name=f"feats_sb{piece}") for piece in pieces]
+        for piece in pieces:
+            queue = nc.sync if piece % 2 == 0 else nc.scalar
+            queue.dma_start(feats_sb[piece][:], feats[:, piece * PIECE : (piece + 1) * PIECE])
         offsets = held.tile([P, N // PER_COLUMN], U16, name="offsets")
         nc.sync.dma_start(offsets[:], offs)
         w_emb_sb = held.tile([P, M], BF16, name="w_emb_sb")
         nc.scalar.dma_start(w_emb_sb[:], w_emb)
         table_sb = held.tile([P, STATIONS], BF16, name="table_sb")
         nc.sync.dma_start(table_sb[:], table)
-        bias = [held.tile([P, 1], F32, name=f"bias{h}") for h in range(M // P)]
-        for h in range(M // P):
+        bias = [held.tile([P, 1], F32, name=f"bias{h}") for h in halves]
+        for h in halves:
             nc.scalar.dma_start(bias[h][:], b[h * P : (h + 1) * P, :])
 
-        blocks = [(piece, h) for piece in range(N // PIECE) for h in range(M // P)]
+        blocks = [(piece, h) for piece in pieces for h in halves]
         bank = {block: banks.tile([P, PIECE], F32, name=f"bank{block[0]}{block[1]}") for block in blocks}
+
+        zeros = held.tile([P, PIECE], BF16, name="zeros")
+        nc.vector.memset(zeros[:], 0.0)
+        for turn in range(WARM_UPS):
+            nc.tensor.matmul(bank[blocks[-1]][:], zeros[:, 0:P], zeros[:], start=True, stop=True)
 
         for piece, h in blocks:
             nc.tensor.matmul(
-                bank[piece, h][:],
-                w_feat_sb[:, h * P : (h + 1) * P],
-                feats_sb[:, piece * PIECE : (piece + 1) * PIECE],
-                start=True,
-                stop=False,
+                bank[piece, h][:], w_feat_sb[:, h * P : (h + 1) * P], feats_sb[piece][:], start=True, stop=False
             )
         for piece, h in blocks:
             piece_offsets = offsets[:, piece * (PIECE // PER_COLUMN) : (piece + 1) * (PIECE // PER_COLUMN)]
@@ -53,8 +57,13 @@ def tile_spaceattn_kernel(tc, table, w_emb, feats, w_feat, b, offs, out):
                 start=False,
                 stop=True,
             )
-            result = results.tile([P, PIECE], F32, name="result")
-            nc.vector.tensor_scalar(
-                out=result[:], in0=bank[piece, h][:], scalar1=bias[h][:], scalar2=None, op0=mybir.AluOpType.add
-            )
+            result = held.tile([P, PIECE], F32, name=f"result{piece}{h}")
+            if h == 0:
+                nc.vector.tensor_scalar(
+                    out=result[:], in0=bank[piece, h][:], scalar1=bias[h][:], scalar2=None, op0=mybir.AluOpType.add
+                )
+            else:
+                nc.scalar.activation(
+                    out=result[:], in_=bank[piece, h][:], func=mybir.ActivationFunctionType.Identity, bias=bias[h][:]
+                )
             nc.sync.dma_start(out[h * P : (h + 1) * P, piece * PIECE : (piece + 1) * PIECE], result[:])

@@ -43,6 +43,8 @@ def tile_spaceattn_kernel(tc, table, w_emb, feats, w_feat, b, offs, out):
         nc.vector.memset(zeros[:], 0.0)
         for turn in range(WARM_UPS):
             nc.tensor.matmul(bank[blocks[-1]][:], zeros[:, 0:P], zeros[:], start=True, stop=True)
+        primed = held.tile([P, 1], F32, name="primed")
+        nc.scalar.activation(out=primed[:], in_=zeros[:, 0:1], func=mybir.ActivationFunctionType.Identity)
 
         for piece, h in blocks:
             nc.tensor.matmul(

@@ -8,8 +8,6 @@ M = 256
 N = 1024
 PIECE = 256
 PER_COLUMN = 16
-WARM_UPS = 5
-
 FLOPS = 2 * M * N * (P + P)
 
 
@@ -39,12 +37,10 @@ def tile_spaceattn_kernel(tc, table, w_emb, feats, w_feat, b, offs, out):
         blocks = [(piece, h) for piece in pieces for h in halves]
         bank = {block: banks.tile([P, PIECE], F32, name=f"bank{block[0]}{block[1]}") for block in blocks}
 
-        zeros = held.tile([P, PIECE], BF16, name="zeros")
-        nc.vector.memset(zeros[:], 0.0)
-        for turn in range(WARM_UPS):
-            nc.tensor.matmul(bank[blocks[-1]][:], zeros[:, 0:P], zeros[:], start=True, stop=True)
+        zero = held.tile([P, 1], F32, name="zero")
+        nc.vector.memset(zero[:], 0.0)
         primed = held.tile([P, 1], F32, name="primed")
-        nc.scalar.activation(out=primed[:], in_=zeros[:, 0:1], func=mybir.ActivationFunctionType.Identity)
+        nc.scalar.activation(out=primed[:], in_=zero[:], func=mybir.ActivationFunctionType.Identity)
 
         for piece, h in blocks:
             nc.tensor.matmul(

@@ -8,6 +8,8 @@ M = 256
 N = 1024
 PIECE = 256
 PER_COLUMN = 16
+WARM_UPS = 5
+
 FLOPS = 2 * M * N * (P + P)
 
 
@@ -20,10 +22,9 @@ def tile_spaceattn_kernel(tc, table, w_emb, feats, w_feat, b, offs, out):
     ):
         w_feat_sb = held.tile([P, M], BF16, name="w_feat_sb")
         nc.scalar.dma_start(w_feat_sb[:], w_feat)
-        feats_sb = [held.tile([P, PIECE], BF16, name=f"feats_sb{piece}") for piece in pieces]
-        for piece in pieces:
-            queue = nc.sync if piece % 2 == 0 else nc.scalar
-            queue.dma_start(feats_sb[piece][:], feats[:, piece * PIECE : (piece + 1) * PIECE])
+        feats_sb = held.tile([P, N], BF16, name="feats_sb")
+        nc.sync.dma_start(feats_sb[:, 0 : N // 2], feats[:, 0 : N // 2])
+        nc.scalar.dma_start(feats_sb[:, N // 2 : N], feats[:, N // 2 : N])
         offsets = held.tile([P, N // PER_COLUMN], U16, name="offsets")
         nc.sync.dma_start(offsets[:], offs)
         w_emb_sb = held.tile([P, M], BF16, name="w_emb_sb")
@@ -37,14 +38,20 @@ def tile_spaceattn_kernel(tc, table, w_emb, feats, w_feat, b, offs, out):
         blocks = [(piece, h) for piece in pieces for h in halves]
         bank = {block: banks.tile([P, PIECE], F32, name=f"bank{block[0]}{block[1]}") for block in blocks}
 
-        zero = held.tile([P, 1], F32, name="zero")
-        nc.vector.memset(zero[:], 0.0)
+        zeros = held.tile([P, PIECE], BF16, name="zeros")
+        nc.vector.memset(zeros[:], 0.0)
+        for turn in range(WARM_UPS):
+            nc.tensor.matmul(bank[blocks[-1]][:], zeros[:, 0:P], zeros[:], start=True, stop=True)
         primed = held.tile([P, 1], F32, name="primed")
-        nc.scalar.activation(out=primed[:], in_=zero[:], func=mybir.ActivationFunctionType.Identity)
+        nc.scalar.activation(out=primed[:], in_=zeros[:, 0:1], func=mybir.ActivationFunctionType.Identity)
 
         for piece, h in blocks:
             nc.tensor.matmul(
-                bank[piece, h][:], w_feat_sb[:, h * P : (h + 1) * P], feats_sb[piece][:], start=True, stop=False
+                bank[piece, h][:],
+                w_feat_sb[:, h * P : (h + 1) * P],
+                feats_sb[:, piece * PIECE : (piece + 1) * PIECE],
+                start=True,
+                stop=False,
             )
         for piece, h in blocks:
             piece_offsets = offsets[:, piece * (PIECE // PER_COLUMN) : (piece + 1) * (PIECE // PER_COLUMN)]

@@ -63,7 +63,7 @@ def tile_spaceattn_kernel(tc, table, w_emb, feats, w_feat, b, offs, out):
                 stop=True,
             )
             result = held.tile([P, PIECE], F32, name=f"result{piece}{h}")
-            if h == 0:
+            if h == 1:
                 nc.vector.tensor_scalar(
                     out=result[:], in0=bank[piece, h][:], scalar1=bias[h][:], scalar2=None, op0=mybir.AluOpType.add
                 )

@@ -8,6 +8,7 @@ M = 256
 N = 1024
 PIECE = 256
 PER_COLUMN = 16
+QUADRANT = 32
 WARM_UPS = 5
 
 FLOPS = 2 * M * N * (P + P)
@@ -38,10 +39,12 @@ def tile_spaceattn_kernel(tc, table, w_emb, feats, w_feat, b, offs, out):
         blocks = [(piece, h) for piece in pieces for h in halves]
         bank = {block: banks.tile([P, PIECE], F32, name=f"bank{block[0]}{block[1]}") for block in blocks}
 
-        zeros = held.tile([P, PIECE], BF16, name="zeros")
+        zeros = held.tile([P, QUADRANT], BF16, name="zeros")
         nc.vector.memset(zeros[:], 0.0)
         for turn in range(WARM_UPS):
-            nc.tensor.matmul(bank[blocks[-1]][:], zeros[:, 0:P], zeros[:], start=True, stop=True)
+            nc.tensor.matmul(
+                bank[blocks[-1]][0:QUADRANT, :], zeros[:], zeros[:, 0:1].to_broadcast([P, PIECE]), start=True, stop=True
+            )
         primed = held.tile([P, 1], F32, name="primed")
         nc.scalar.activation(out=primed[:], in_=zeros[:, 0:1], func=mybir.ActivationFunctionType.Identity)
 

@@ -24,7 +24,8 @@ def tile_spaceattn_kernel(tc, table, w_emb, feats, w_feat, b, offs, out):
         w_feat_sb = held.tile([P, M], BF16, name="w_feat_sb")
         nc.scalar.dma_start(w_feat_sb[:], w_feat)
         feats_sb = held.tile([P, N], BF16, name="feats_sb")
-        nc.sync.dma_start(feats_sb[:, 0 : N // 2], feats[:, 0 : N // 2])
+        nc.sync.dma_start(feats_sb[:, 0:PIECE], feats[:, 0:PIECE])
+        nc.sync.dma_start(feats_sb[:, PIECE : N // 2], feats[:, PIECE : N // 2])
         nc.scalar.dma_start(feats_sb[:, N // 2 : N], feats[:, N // 2 : N])
         offsets = held.tile([P, N // PER_COLUMN], U16, name="offsets")
         nc.sync.dma_start(offsets[:], offs)
@@ -34,7 +35,7 @@ def tile_spaceattn_kernel(tc, table, w_emb, feats, w_feat, b, offs, out):
         nc.sync.dma_start(table_sb[:], table)
         bias = [held.tile([P, 1], F32, name=f"bias{h}") for h in halves]
         for h in halves:
-            nc.scalar.dma_start(bias[h][:], b[h * P : (h + 1) * P, :])
+            nc.gpsimd.dma_start(bias[h][:], b[h * P : (h + 1) * P, :])
 
         blocks = [(piece, h) for piece in pieces for h in halves]
         bank = {block: banks.tile([P, PIECE], F32, name=f"bank{block[0]}{block[1]}") for block in blocks}

@@ -9,6 +9,7 @@ N = 1024
 PIECE = 256
 PER_COLUMN = 16
 QUADRANT = 32
+SQUARE = 32
 WARM_UPS = 5
 
 FLOPS = 2 * M * N * (P + P)
@@ -21,6 +22,9 @@ def tile_spaceattn_kernel(tc, table, w_emb, feats, w_feat, b, offs, out):
         tc.tile_pool(name="held", bufs=1) as held,
         tc.psum_pool(name="banks", bufs=1) as banks,
     ):
+        zeros = held.tile([P, QUADRANT], BF16, name="zeros")
+        nc.vector.memset(zeros[:], 0.0)
+
         w_feat_sb = held.tile([P, M], BF16, name="w_feat_sb")
         nc.scalar.dma_start(w_feat_sb[:], w_feat)
         feats_sb = held.tile([P, N], BF16, name="feats_sb")
@@ -33,15 +37,20 @@ def tile_spaceattn_kernel(tc, table, w_emb, feats, w_feat, b, offs, out):
         nc.scalar.dma_start(w_emb_sb[:], w_emb)
         table_sb = held.tile([P, STATIONS], BF16, name="table_sb")
         nc.sync.dma_start(table_sb[:], table)
-        bias = [held.tile([P, 1], F32, name=f"bias{h}") for h in halves]
+        b_lying = held.tile([P, (M // P) * SQUARE], F32, name="b_lying", align_bytes=64)
+        nc.vector.memset(b_lying[:], 0.0)
+        nc.sync.dma_start(
+            b_lying[0:P:SQUARE, :].rearrange("q (h i) -> q h i", i=SQUARE),
+            b.rearrange("(h q i) o -> q h (i o)", q=P // SQUARE, i=SQUARE),
+        )
+        b_upright = held.tile([P, (M // P) * SQUARE], F32, name="b_upright", align_bytes=64)
         for h in halves:
-            nc.gpsimd.dma_start(bias[h][:], b[h * P : (h + 1) * P, :])
+            nc.vector.transpose(b_upright[:, h * SQUARE : (h + 1) * SQUARE], b_lying[:, h * SQUARE : (h + 1) * SQUARE])
+        bias = [b_upright[:, h * SQUARE : h * SQUARE + 1] for h in halves]
 
         blocks = [(piece, h) for piece in pieces for h in halves]
         bank = {block: banks.tile([P, PIECE], F32, name=f"bank{block[0]}{block[1]}") for block in blocks}
 
-        zeros = held.tile([P, QUADRANT], BF16, name="zeros")
-        nc.vector.memset(zeros[:], 0.0)
         for turn in range(WARM_UPS):
             nc.tensor.matmul(
                 bank[blocks[-1]][0:QUADRANT, :], zeros[:], zeros[:, 0:1].to_broadcast([P, PIECE]), start=True, stop=True
@@ -69,10 +78,10 @@ def tile_spaceattn_kernel(tc, table, w_emb, feats, w_feat, b, offs, out):
             result = held.tile([P, PIECE], F32, name=f"result{piece}{h}")
             if h == 1:
                 nc.vector.tensor_scalar(
-                    out=result[:], in0=bank[piece, h][:], scalar1=bias[h][:], scalar2=None, op0=mybir.AluOpType.add
+                    out=result[:], in0=bank[piece, h][:], scalar1=bias[h], scalar2=None, op0=mybir.AluOpType.add
                 )
             else:
                 nc.scalar.activation(
-                    out=result[:], in_=bank[piece, h][:], func=mybir.ActivationFunctionType.Identity, bias=bias[h][:]
+                    out=result[:], in_=bank[piece, h][:], func=mybir.ActivationFunctionType.Identity, bias=bias[h]
                 )
             nc.sync.dma_start(out[h * P : (h + 1) * P, piece * PIECE : (piece + 1) * PIECE], result[:])

import concourse.mybir as mybir

BF16, F32, U16 = mybir.dt.bfloat16, mybir.dt.float32, mybir.dt.uint16

P = 128
STATIONS = 512
M = 256
N = 1024
PIECE = 256
PER_COLUMN = 16
QUADRANT = 32
SQUARE = 32
WARM_UPS = 5

FLOPS = 2 * M * N * (P + P)


def tile_spaceattn_kernel(tc, table, w_emb, feats, w_feat, b, offs, out):
    nc = tc.nc
    pieces, halves = range(N // PIECE), range(M // P)
    with (
        tc.tile_pool(name="held", bufs=1) as held,
        tc.psum_pool(name="banks", bufs=1) as banks,
    ):
        zeros = held.tile([P, QUADRANT], BF16, name="zeros")
        nc.vector.memset(zeros[:], 0.0)

        w_feat_sb = held.tile([P, M], BF16, name="w_feat_sb")
        nc.scalar.dma_start(w_feat_sb[:], w_feat)
        feats_sb = held.tile([P, N], BF16, name="feats_sb")
        nc.sync.dma_start(feats_sb[:, 0:PIECE], feats[:, 0:PIECE])
        nc.sync.dma_start(feats_sb[:, PIECE : N // 2], feats[:, PIECE : N // 2])
        nc.scalar.dma_start(feats_sb[:, N // 2 : N], feats[:, N // 2 : N])
        offsets = held.tile([P, N // PER_COLUMN], U16, name="offsets")
        nc.sync.dma_start(offsets[:], offs)
        w_emb_sb = held.tile([P, M], BF16, name="w_emb_sb")
        nc.scalar.dma_start(w_emb_sb[:], w_emb)
        table_sb = held.tile([P, STATIONS], BF16, name="table_sb")
        nc.sync.dma_start(table_sb[:], table)
        b_lying = held.tile([P, (M // P) * SQUARE], F32, name="b_lying", align_bytes=64)
        nc.vector.memset(b_lying[:], 0.0)
        nc.sync.dma_start(
            b_lying[0:P:SQUARE, :].rearrange("q (h i) -> q h i", i=SQUARE),
            b.rearrange("(h q i) o -> q h (i o)", q=P // SQUARE, i=SQUARE),
        )
        b_upright = held.tile([P, (M // P) * SQUARE], F32, name="b_upright", align_bytes=64)
        for h in halves:
            nc.vector.transpose(b_upright[:, h * SQUARE : (h + 1) * SQUARE], b_lying[:, h * SQUARE : (h + 1) * SQUARE])
        bias = [b_upright[:, h * SQUARE : h * SQUARE + 1] for h in halves]

        blocks = [(piece, h) for piece in pieces for h in halves]
        bank = {block: banks.tile([P, PIECE], F32, name=f"bank{block[0]}{block[1]}") for block in blocks}

        for turn in range(WARM_UPS):
            nc.tensor.matmul(
                bank[blocks[-1]][0:QUADRANT, :], zeros[:], zeros[:, 0:1].to_broadcast([P, PIECE]), start=True, stop=True
            )
        primed = held.tile([P, 1], F32, name="primed")
        nc.scalar.activation(out=primed[:], in_=zeros[:, 0:1], func=mybir.ActivationFunctionType.Identity)

        for piece, h in blocks:
            nc.tensor.matmul(
                bank[piece, h][:],
                w_feat_sb[:, h * P : (h + 1) * P],
                feats_sb[:, piece * PIECE : (piece + 1) * PIECE],
                start=True,
                stop=False,
            )
        for piece, h in blocks:
            piece_offsets = offsets[:, piece * (PIECE // PER_COLUMN) : (piece + 1) * (PIECE // PER_COLUMN)]
            nc.tensor.matmul(
                bank[piece, h][:],
                w_emb_sb[:, h * P : (h + 1) * P],
                table_sb[:].indirect(piece_offsets),
                start=False,
                stop=True,
            )
            result = held.tile([P, PIECE], F32, name=f"result{piece}{h}")
            if h == 1:
                nc.vector.tensor_scalar(
                    out=result[:], in0=bank[piece, h][:], scalar1=bias[h], scalar2=None, op0=mybir.AluOpType.add
                )
            else:
                nc.scalar.activation(
                    out=result[:], in_=bank[piece, h][:], func=mybir.ActivationFunctionType.Identity, bias=bias[h]
                )
            nc.sync.dma_start(out[h * P : (h + 1) * P, piece * PIECE : (piece + 1) * PIECE], result[:])
